import numpy as np
import ml_dtypes


def mxq(x, axis, fmt="e4m3"):
    dtype, down = {"e4m3": (ml_dtypes.float8_e4m3fn, 7), "e5m2": (ml_dtypes.float8_e5m2, 14)}[fmt]
    v = np.moveaxis(np.asarray(x, np.float32).astype(ml_dtypes.bfloat16).astype(np.float64), axis, -1)
    blocks = v.reshape(v.shape[:-1] + (-1, 32))
    amax = np.abs(blocks).max(-1, keepdims=True)
    byte = np.maximum(np.where(amax > 0, np.frexp(amax)[1] - 1 + 127, 0) - down, 1)
    scale = np.exp2(byte - 127.0)
    codes = (blocks / scale).astype(np.float32).astype(dtype).astype(np.float64)
    return np.moveaxis((codes * scale).reshape(v.shape), -1, axis)


WIDE = False


def mx_kscale(k):
    if not WIDE:
        return np.ones(k)
    levels = np.array([10, -10, 5, -5, 0])
    a = np.random.permutation(np.resize(levels, k // 512 * 4)).reshape(k // 512, 4)
    idx = np.arange(k)
    return np.exp2(a[idx // 512, idx % 128 // 32])


BF16 = ml_dtypes.bfloat16


def bf(x):
    return np.asarray(x, np.float32).astype(BF16)


def f64(x):
    return np.asarray(x).astype(np.float64)


B, T, N, F_IN, F_OUT, K = 1, 4, 512, 1024, 1024, 4


def delay(v, d):
    return np.concatenate([np.zeros((B, d, N, F_OUT)), v], axis=1)


def setup_inputs():
    s = mx_kscale(F_IN)
    return {"X": bf(np.random.standard_normal((B, T, N, F_IN)) * s),
            "S": bf(np.random.standard_normal((N, N)) / np.sqrt(N)),
            "w0": bf(np.random.standard_normal((F_OUT, F_IN)) / np.sqrt(F_IN) / s),
            "w1": bf(np.random.standard_normal((F_OUT, F_IN)) / np.sqrt(F_IN) / s)}


def reference(X, S, w0, w1):
    X = f64(X)
    z1 = mxq(f64(S), 1, "e4m3") @ mxq(X[:, :T - 1], 2, "e4m3")
    t0 = mxq(X, 3, "e4m3") @ mxq(f64(w0), 1, "e4m3").T
    t1 = mxq(z1, 3, "e4m3") @ mxq(f64(w1), 1, "e4m3").T
    return t0 + delay(t1, 1)

@@ -1,0 +1,177 @@
+from contextlib import ExitStack
+
+import concourse.mybir as mybir
+from concourse.masks import make_identity
+
+BF16 = mybir.dt.bfloat16
+F32 = mybir.dt.float32
+U32 = mybir.dt.uint32
+U8 = mybir.dt.uint8
+FP8X4 = mybir.dt.float8_e4m3fn_x4
+
+P = 128
+PACK = 4
+K_PASS = P * PACK
+BANK = 512
+
+STEPS = 4
+NODES = 512
+F_IN = 1024
+F_OUT = 1024
+BLOCKS = NODES // P
+F_PASSES = F_IN // K_PASS
+HALVES = F_OUT // BANK
+
+FLOPS = 2 * ((STEPS - 1) * NODES * NODES * F_IN + (2 * STEPS - 1) * NODES * F_IN * F_OUT)
+
+
+def tile_stgnnlayer_pa_kernel(tc, X, S, w0, w1, out):
+    nc = tc.nc
+    with ExitStack() as ctx:
+        inputs = ctx.enter_context(tc.tile_pool(name="inputs", bufs=1))
+        keep = ctx.enter_context(tc.tile_pool(name="keep", bufs=1))
+        stage = ctx.enter_context(tc.tile_pool(name="stage", bufs=6))
+        results = ctx.enter_context(tc.tile_pool(name="results", bufs=8))
+        psum = ctx.enter_context(tc.psum_pool(name="psum", bufs=8))
+
+        s_sb = inputs.tile([P, BLOCKS, NODES], BF16)
+        x_sb = [inputs.tile([P, BLOCKS, F_IN], BF16, name="x_sb%d" % t) for t in range(STEPS)]
+        w_sb = [inputs.tile([P, BLOCKS, F_IN], BF16, name="w_sb%d" % i) for i in range(2 * HALVES)]
+
+        def load_x(t):
+            nc.sync.dma_start(out=x_sb[t][:], in_=X[0, t].rearrange("(p j) f -> p j f", j=BLOCKS))
+
+        def load_w(w, tap, h):
+            rows = w[h * BANK : (h + 1) * BANK, :]
+            nc.sync.dma_start(out=w_sb[tap * HALVES + h][:], in_=rows.rearrange("(c p) f -> p c f", p=P))
+
+        nc.sync.dma_start(out=s_sb[:], in_=S.rearrange("(p j) n -> p j n", j=BLOCKS))
+        load_x(0)
+        load_w(w0, 0, 0)
+        load_w(w0, 0, 1)
+        load_x(1)
+        load_w(w1, 1, 0)
+        load_w(w1, 1, 1)
+        load_x(2)
+        load_x(3)
+
+        ident = keep.tile([P, P], F32)
+        make_identity(nc, ident[:])
+
+        s_codes = keep.tile([P, NODES], U32, align_bytes=64)
+        s_scales = keep.tile([P, NODES], U8, align_bytes=64)
+        xn_codes = keep.tile([P, STEPS - 1, F_IN], U32, align_bytes=64)
+        xn_scales = keep.tile([P, STEPS - 1, F_IN], U8, align_bytes=64)
+        xf_codes = keep.tile([P, STEPS, F_PASSES, NODES], U32, align_bytes=64)
+        xf_scales = keep.tile([P, STEPS, F_PASSES, NODES], U8, align_bytes=64)
+        z_codes = keep.tile([P, STEPS - 1, F_PASSES, NODES], U32, align_bytes=64)
+        z_scales = keep.tile([P, STEPS - 1, F_PASSES, NODES], U8, align_bytes=64)
+        w_codes = keep.tile([P, 2, F_PASSES, F_OUT], U32, align_bytes=64)
+        w_scales = keep.tile([P, 2, F_PASSES, F_OUT], U8, align_bytes=64)
+
+        def quantise(grouped, codes, scales):
+            nc.vector.quantize_mx(
+                out=codes.bitcast(FP8X4),
+                scales=scales,
+                in_=grouped[:].rearrange("p c v -> p (c v)"),
+            )
+
+        def transpose_and_quantise(words, codes, scales):
+            grouped = stage.tile([P, BLOCKS * P, PACK], BF16, align_bytes=64)
+            grouped_words = grouped[:].bitcast(F32)
+            for pair in range(2):
+                bank = psum.tile([P, BANK], F32, tag="bank")
+                planes = bank[:].rearrange("p (u b c) -> p u b c", u=2, b=2)
+                for u in range(2):
+                    for b in range(2):
+                        nc.tensor.transpose(planes[:, u, b, :], words[:, 2 * pair + b, u, :], ident[:])
+                copy = nc.vector.tensor_copy if pair == 0 else nc.scalar.copy
+                copy(
+                    out=grouped_words[:, 2 * P * pair : 2 * P * (pair + 1), :],
+                    in_=bank[:].rearrange("p (u c) -> p c u", u=2),
+                )
+            quantise(grouped, codes, scales)
+
+        def prepare_s():
+            words = s_sb[:].bitcast(F32).rearrange("p j (q u) -> p j u q", u=2)
+            transpose_and_quantise(words, s_codes[:], s_scales[:])
+
+        def prepare_w(tap, h):
+            cols = slice(h * BANK, (h + 1) * BANK)
+            words = w_sb[tap * HALVES + h][:].bitcast(F32).rearrange("p c (g u q) -> p c g u q", g=F_PASSES, u=2)
+            for g in range(F_PASSES):
+                transpose_and_quantise(words[:, :, g, :, :], w_codes[:, tap, g, cols], w_scales[:, tap, g, cols])
+
+        def prepare_x(t):
+            words = x_sb[t][:].bitcast(F32).rearrange("p j (g u q) -> p j g u q", g=F_PASSES, u=2)
+            for g in range(F_PASSES):
+                transpose_and_quantise(words[:, :, g, :, :], xf_codes[:, t, g, :], xf_scales[:, t, g, :])
+            if t == STEPS - 1:
+                return
+            for g in range(F_PASSES):
+                cols = slice(g * K_PASS, (g + 1) * K_PASS)
+                grouped = stage.tile([P, K_PASS, PACK], BF16, align_bytes=64)
+                nc.vector.tensor_copy(
+                    out=grouped[:].rearrange("p (u e q) j -> p u e q j", u=2, e=2),
+                    in_=x_sb[t][:, :, cols].rearrange("p j (u q e) -> p u e q j", u=2, e=2),
+                )
+                quantise(grouped, xn_codes[:, t, cols], xn_scales[:, t, cols])
+
+        def graph_shift(t):
+            for g in range(F_PASSES):
+                grouped = stage.tile([P, NODES, PACK], BF16, align_bytes=64)
+                for j in range(BLOCKS):
+                    nodes = slice(j * P, (j + 1) * P)
+                    bank = psum.tile([P, BANK], F32, tag="bank")
+                    planes = bank[:].rearrange("p (v c) -> p v c", v=PACK)
+                    for v in range(PACK):
+                        feats = slice(g * K_PASS + v * P, g * K_PASS + (v + 1) * P)
+                        nc.tensor.matmul_mx(
+                            out=planes[:, v, :],
+                            lhsT=xn_codes[:, t, feats].bitcast(FP8X4),
+                            lhsT_scale=xn_scales[:, t, feats],
+                            rhs=s_codes[:, nodes].bitcast(FP8X4),
+                            rhs_scale=s_scales[:, nodes],
+                            start=True,
+                            stop=True,
+                        )
+                    nc.scalar.copy(out=grouped[:, nodes, :], in_=planes.rearrange("p v c -> p c v"))
+                quantise(grouped, z_codes[:, t, g, :], z_scales[:, t, g, :])
+
+        def taps(t, h):
+            cols = slice(h * BANK, (h + 1) * BANK)
+            y_rows = out[0, t].rearrange("(p j) o -> p j o", j=BLOCKS)
+            for j in range(BLOCKS):
+                nodes = slice(j * P, (j + 1) * P)
+                passes = [(xf_codes[:, t, g, nodes], xf_scales[:, t, g, nodes], 0, g) for g in range(F_PASSES)]
+                if t > 0:
+                    passes += [
+                        (z_codes[:, t - 1, g, nodes], z_scales[:, t - 1, g, nodes], 1, g) for g in range(F_PASSES)
+                    ]
+                bank = psum.tile([P, BANK], F32, tag="bank")
+                for i, (codes, scales, tap, g) in enumerate(passes):
+                    nc.tensor.matmul_mx(
+                        out=bank[:],
+                        lhsT=codes.bitcast(FP8X4),
+                        lhsT_scale=scales,
+                        rhs=w_codes[:, tap, g, cols].bitcast(FP8X4),
+                        rhs_scale=w_scales[:, tap, g, cols],
+                        start=(i == 0),
+                        stop=(i == len(passes) - 1),
+                    )
+                y_sb = results.tile([P, BANK], F32)
+                nc.scalar.copy(out=y_sb[:], in_=bank[:])
+                nc.sync.dma_start(out=y_rows[:, j, cols], in_=y_sb[:])
+
+        prepare_s()
+        prepare_x(0)
+        prepare_w(0, 0)
+        for t in range(STEPS):
+            for h in range(HALVES):
+                following = t * HALVES + h + 1
+                if following < 2 * HALVES:
+                    prepare_w(following // HALVES, following % HALVES)
+                taps(t, h)
+                if h == 0 and t + 1 < STEPS:
+                    graph_shift(t)
+                    prepare_x(t + 1)

@@ -30,9 +30,10 @@ def tile_stgnnlayer_pa_kernel(tc, X, S, w0, w1, out):
     with ExitStack() as ctx:
         inputs = ctx.enter_context(tc.tile_pool(name="inputs", bufs=1))
         keep = ctx.enter_context(tc.tile_pool(name="keep", bufs=1))
-        stage = ctx.enter_context(tc.tile_pool(name="stage", bufs=6))
+        stage = ctx.enter_context(tc.tile_pool(name="stage", bufs=8))
         results = ctx.enter_context(tc.tile_pool(name="results", bufs=8))
         psum = ctx.enter_context(tc.psum_pool(name="psum", bufs=8))
+        ctx.enter_context(tc.manual_schedule())
 
         s_sb = inputs.tile([P, BLOCKS, NODES], BF16)
         x_sb = [inputs.tile([P, BLOCKS, F_IN], BF16, name="x_sb%d" % t) for t in range(STEPS)]
@@ -45,10 +46,10 @@ def tile_stgnnlayer_pa_kernel(tc, X, S, w0, w1, out):
             rows = w[h * BANK : (h + 1) * BANK, :]
             nc.sync.dma_start(out=w_sb[tap * HALVES + h][:], in_=rows.rearrange("(c p) f -> p c f", p=P))
 
-        nc.sync.dma_start(out=s_sb[:], in_=S.rearrange("(p j) n -> p j n", j=BLOCKS))
         load_x(0)
         load_w(w0, 0, 0)
         load_w(w0, 0, 1)
+        nc.sync.dma_start(out=s_sb[:], in_=S.rearrange("(p j) n -> p j n", j=BLOCKS))
         load_x(1)
         load_w(w1, 1, 0)
         load_w(w1, 1, 1)
@@ -69,6 +70,9 @@ def tile_stgnnlayer_pa_kernel(tc, X, S, w0, w1, out):
         w_codes = keep.tile([P, 2, F_PASSES, F_OUT], U32, align_bytes=64)
         w_scales = keep.tile([P, 2, F_PASSES, F_OUT], U8, align_bytes=64)
 
+        def copy_for_block(j):
+            return nc.scalar.copy if j % 2 == 0 else nc.vector.tensor_copy
+
         def quantise(grouped, codes, scales):
             nc.vector.quantize_mx(
                 out=codes.bitcast(FP8X4),
@@ -85,8 +89,7 @@ def tile_stgnnlayer_pa_kernel(tc, X, S, w0, w1, out):
                 for u in range(2):
                     for b in range(2):
                         nc.tensor.transpose(planes[:, u, b, :], words[:, 2 * pair + b, u, :], ident[:])
-                copy = nc.vector.tensor_copy if pair == 0 else nc.scalar.copy
-                copy(
+                nc.scalar.copy(
                     out=grouped_words[:, 2 * P * pair : 2 * P * (pair + 1), :],
                     in_=bank[:].rearrange("p (u c) -> p c u", u=2),
                 )
@@ -102,20 +105,19 @@ def tile_stgnnlayer_pa_kernel(tc, X, S, w0, w1, out):
             for g in range(F_PASSES):
                 transpose_and_quantise(words[:, :, g, :, :], w_codes[:, tap, g, cols], w_scales[:, tap, g, cols])
 
-        def prepare_x(t):
+        def prepare_x_for_taps(t):
             words = x_sb[t][:].bitcast(F32).rearrange("p j (g u q) -> p j g u q", g=F_PASSES, u=2)
             for g in range(F_PASSES):
                 transpose_and_quantise(words[:, :, g, :, :], xf_codes[:, t, g, :], xf_scales[:, t, g, :])
-            if t == STEPS - 1:
-                return
-            for g in range(F_PASSES):
-                cols = slice(g * K_PASS, (g + 1) * K_PASS)
-                grouped = stage.tile([P, K_PASS, PACK], BF16, align_bytes=64)
-                nc.vector.tensor_copy(
-                    out=grouped[:].rearrange("p (u e q) j -> p u e q j", u=2, e=2),
-                    in_=x_sb[t][:, :, cols].rearrange("p j (u q e) -> p u e q j", u=2, e=2),
-                )
-                quantise(grouped, xn_codes[:, t, cols], xn_scales[:, t, cols])
+
+        def prepare_x_for_shift(t, g):
+            cols = slice(g * K_PASS, (g + 1) * K_PASS)
+            grouped = stage.tile([P, K_PASS, PACK], BF16, align_bytes=64)
+            nc.vector.tensor_copy(
+                out=grouped[:].rearrange("p (u e q) j -> p u e q j", u=2, e=2),
+                in_=x_sb[t][:, :, cols].rearrange("p j (u q e) -> p u e q j", u=2, e=2),
+            )
+            quantise(grouped, xn_codes[:, t, cols], xn_scales[:, t, cols])
 
         def graph_shift(t):
             for g in range(F_PASSES):
@@ -135,7 +137,7 @@ def tile_stgnnlayer_pa_kernel(tc, X, S, w0, w1, out):
                             start=True,
                             stop=True,
                         )
-                    nc.scalar.copy(out=grouped[:, nodes, :], in_=planes.rearrange("p v c -> p c v"))
+                    copy_for_block(j)(out=grouped[:, nodes, :], in_=planes.rearrange("p v c -> p c v"))
                 quantise(grouped, z_codes[:, t, g, :], z_scales[:, t, g, :])
 
         def taps(t, h):
@@ -160,18 +162,24 @@ def tile_stgnnlayer_pa_kernel(tc, X, S, w0, w1, out):
                         stop=(i == len(passes) - 1),
                     )
                 y_sb = results.tile([P, BANK], F32)
-                nc.scalar.copy(out=y_sb[:], in_=bank[:])
+                copy_for_block(j)(out=y_sb[:], in_=bank[:])
                 nc.sync.dma_start(out=y_rows[:, j, cols], in_=y_sb[:])
 
-        prepare_s()
-        prepare_x(0)
+        prepare_x_for_shift(0, 0)
+        prepare_x_for_taps(0)
         prepare_w(0, 0)
+        prepare_x_for_shift(0, 1)
+        prepare_w(0, 1)
+        prepare_s()
         for t in range(STEPS):
             for h in range(HALVES):
-                following = t * HALVES + h + 1
-                if following < 2 * HALVES:
-                    prepare_w(following // HALVES, following % HALVES)
                 taps(t, h)
                 if h == 0 and t + 1 < STEPS:
+                    prepare_x_for_taps(t + 1)
+                if t == 0:
+                    prepare_w(1, h)
+                if h == 0 and t + 1 < STEPS:
                     graph_shift(t)
-                    prepare_x(t + 1)
+                if h == 1 and t + 2 < STEPS:
+                    for g in range(F_PASSES):
+                        prepare_x_for_shift(t + 1, g)

@@ -22,6 +22,9 @@ BLOCKS = NODES // P
 F_PASSES = F_IN // K_PASS
 HALVES = F_OUT // BANK
 
+WARM_START = 8
+WARM_FILL = 3
+
 FLOPS = 2 * ((STEPS - 1) * NODES * NODES * F_IN + (2 * STEPS - 1) * NODES * F_IN * F_OUT)
 
 
@@ -58,6 +61,13 @@ def tile_stgnnlayer_pa_kernel(tc, X, S, w0, w1, out):
 
         ident = keep.tile([P, P], F32)
         make_identity(nc, ident[:])
+        zeros = keep.tile([P, BANK], BF16)
+        nc.vector.memset(zeros[:], 0.0)
+
+        def keep_clock_up(count):
+            unread = psum.tile([P, BANK], F32, tag="bank")
+            for i in range(count):
+                nc.tensor.matmul(out=unread[:], lhsT=zeros[:, :P], rhs=zeros[:], start=True, stop=True)
 
         s_codes = keep.tile([P, NODES], U32, align_bytes=64)
         s_scales = keep.tile([P, NODES], U8, align_bytes=64)
@@ -165,21 +175,24 @@ def tile_stgnnlayer_pa_kernel(tc, X, S, w0, w1, out):
                 copy_for_block(j)(out=y_sb[:], in_=bank[:])
                 nc.sync.dma_start(out=y_rows[:, j, cols], in_=y_sb[:])
 
+        keep_clock_up(WARM_START)
         prepare_x_for_shift(0, 0)
         prepare_x_for_taps(0)
+        keep_clock_up(WARM_FILL)
         prepare_w(0, 0)
+        keep_clock_up(WARM_FILL)
         prepare_x_for_shift(0, 1)
         prepare_w(0, 1)
+        keep_clock_up(WARM_FILL)
         prepare_s()
         for t in range(STEPS):
             for h in range(HALVES):
                 taps(t, h)
                 if h == 0 and t + 1 < STEPS:
                     prepare_x_for_taps(t + 1)
+                    graph_shift(t)
                 if t == 0:
                     prepare_w(1, h)
-                if h == 0 and t + 1 < STEPS:
-                    graph_shift(t)
                 if h == 1 and t + 2 < STEPS:
                     for g in range(F_PASSES):
                         prepare_x_for_shift(t + 1, g)

@@ -120,18 +120,24 @@ def tile_stgnnlayer_pa_kernel(tc, X, S, w0, w1, out):
             for g in range(F_PASSES):
                 transpose_and_quantise(words[:, :, g, :, :], xf_codes[:, t, g, :], xf_scales[:, t, g, :])
 
-        def prepare_x_for_shift(t, g):
-            cols = slice(g * K_PASS, (g + 1) * K_PASS)
-            grouped = stage.tile([P, K_PASS, PACK], BF16, align_bytes=64)
-            nc.vector.tensor_copy(
-                out=grouped[:].rearrange("p (u e q) j -> p u e q j", u=2, e=2),
-                in_=x_sb[t][:, :, cols].rearrange("p j (u q e) -> p u e q j", u=2, e=2),
-            )
-            quantise(grouped, xn_codes[:, t, cols], xn_scales[:, t, cols])
+        def prepare_x_for_shift(t):
+            halves = []
+            for g in range(F_PASSES):
+                grouped = stage.tile([P, K_PASS, PACK], BF16, align_bytes=64)
+                nc.vector.tensor_copy(
+                    out=grouped[:].rearrange("p (u e q) j -> p u e q j", u=2, e=2),
+                    in_=x_sb[t][:, :, g * K_PASS : (g + 1) * K_PASS].rearrange("p j (u q e) -> p u e q j", u=2, e=2),
+                )
+                halves.append(grouped)
+            for g in range(F_PASSES):
+                cols = slice(g * K_PASS, (g + 1) * K_PASS)
+                quantise(halves[g], xn_codes[:, t, cols], xn_scales[:, t, cols])
 
         def graph_shift(t):
+            halves = []
             for g in range(F_PASSES):
                 grouped = stage.tile([P, NODES, PACK], BF16, align_bytes=64)
+                halves.append(grouped)
                 for j in range(BLOCKS):
                     nodes = slice(j * P, (j + 1) * P)
                     bank = psum.tile([P, BANK], F32, tag="bank")
@@ -148,7 +154,8 @@ def tile_stgnnlayer_pa_kernel(tc, X, S, w0, w1, out):
                             stop=True,
                         )
                     copy_for_block(j)(out=grouped[:, nodes, :], in_=planes.rearrange("p v c -> p c v"))
-                quantise(grouped, z_codes[:, t, g, :], z_scales[:, t, g, :])
+            for g in range(F_PASSES):
+                quantise(halves[g], z_codes[:, t, g, :], z_scales[:, t, g, :])
 
         def taps(t, h):
             cols = slice(h * BANK, (h + 1) * BANK)
@@ -176,12 +183,11 @@ def tile_stgnnlayer_pa_kernel(tc, X, S, w0, w1, out):
                 nc.sync.dma_start(out=y_rows[:, j, cols], in_=y_sb[:])
 
         keep_clock_up(WARM_START)
-        prepare_x_for_shift(0, 0)
+        prepare_x_for_shift(0)
         prepare_x_for_taps(0)
         keep_clock_up(WARM_FILL)
         prepare_w(0, 0)
         keep_clock_up(WARM_FILL)
-        prepare_x_for_shift(0, 1)
         prepare_w(0, 1)
         keep_clock_up(WARM_FILL)
         prepare_s()
@@ -191,8 +197,7 @@ def tile_stgnnlayer_pa_kernel(tc, X, S, w0, w1, out):
                 if h == 0 and t + 1 < STEPS:
                     prepare_x_for_taps(t + 1)
                     graph_shift(t)
+                if h == 1 and t + 2 < STEPS:
+                    prepare_x_for_shift(t + 1)
                 if t == 0:
                     prepare_w(1, h)
-                if h == 1 and t + 2 < STEPS:
-                    for g in range(F_PASSES):
-                        prepare_x_for_shift(t + 1, g)

@@ -34,16 +34,22 @@ def tile_stgnnlayer_pa_kernel(tc, X, S, w0, w1, out):
         inputs = ctx.enter_context(tc.tile_pool(name="inputs", bufs=1))
         keep = ctx.enter_context(tc.tile_pool(name="keep", bufs=1))
         stage = ctx.enter_context(tc.tile_pool(name="stage", bufs=8))
-        results = ctx.enter_context(tc.tile_pool(name="results", bufs=8))
+        results = ctx.enter_context(tc.tile_pool(name="results", bufs=16))
         psum = ctx.enter_context(tc.psum_pool(name="psum", bufs=8))
         ctx.enter_context(tc.manual_schedule())
+
+        def by_node(matrix):
+            return matrix.rearrange("(u p e) f -> p u e f", u=2, e=2)
+
+        def by_block(tile):
+            return tile[:].rearrange("p (u e) f -> p u e f", u=2)
 
         s_sb = inputs.tile([P, BLOCKS, NODES], BF16)
         x_sb = [inputs.tile([P, BLOCKS, F_IN], BF16, name="x_sb%d" % t) for t in range(STEPS)]
         w_sb = [inputs.tile([P, BLOCKS, F_IN], BF16, name="w_sb%d" % i) for i in range(2 * HALVES)]
 
         def load_x(t):
-            nc.sync.dma_start(out=x_sb[t][:], in_=X[0, t].rearrange("(p j) f -> p j f", j=BLOCKS))
+            nc.sync.dma_start(out=by_block(x_sb[t]), in_=by_node(X[0, t]))
 
         def load_w(w, tap, h):
             rows = w[h * BANK : (h + 1) * BANK, :]
@@ -52,7 +58,7 @@ def tile_stgnnlayer_pa_kernel(tc, X, S, w0, w1, out):
         load_x(0)
         load_w(w0, 0, 0)
         load_w(w0, 0, 1)
-        nc.sync.dma_start(out=s_sb[:], in_=S.rearrange("(p j) n -> p j n", j=BLOCKS))
+        nc.sync.dma_start(out=by_block(s_sb), in_=by_node(S))
         load_x(1)
         load_w(w1, 1, 0)
         load_w(w1, 1, 1)
@@ -106,7 +112,7 @@ def tile_stgnnlayer_pa_kernel(tc, X, S, w0, w1, out):
             quantise(grouped, codes, scales)
 
         def prepare_s():
-            words = s_sb[:].bitcast(F32).rearrange("p j (q u) -> p j u q", u=2)
+            words = s_sb[:].bitcast(F32).rearrange("p j (u q) -> p j u q", u=2)
             transpose_and_quantise(words, s_codes[:], s_scales[:])
 
         def prepare_w(tap, h):
@@ -159,7 +165,7 @@ def tile_stgnnlayer_pa_kernel(tc, X, S, w0, w1, out):
 
         def taps(t, h):
             cols = slice(h * BANK, (h + 1) * BANK)
-            y_rows = out[0, t].rearrange("(p j) o -> p j o", j=BLOCKS)
+            y_rows = by_node(out[0, t])
             for j in range(BLOCKS):
                 nodes = slice(j * P, (j + 1) * P)
                 passes = [(xf_codes[:, t, g, nodes], xf_scales[:, t, g, nodes], 0, g) for g in range(F_PASSES)]
@@ -180,7 +186,7 @@ def tile_stgnnlayer_pa_kernel(tc, X, S, w0, w1, out):
                     )
                 y_sb = results.tile([P, BANK], F32)
                 copy_for_block(j)(out=y_sb[:], in_=bank[:])
-                nc.sync.dma_start(out=y_rows[:, j, cols], in_=y_sb[:])
+                nc.sync.dma_start(out=y_rows[:, j // 2, j % 2, cols], in_=y_sb[:])
 
         keep_clock_up(WARM_START)
         prepare_x_for_shift(0)

@@ -21,9 +21,11 @@ F_OUT = 1024
 BLOCKS = NODES // P
 F_PASSES = F_IN // K_PASS
 HALVES = F_OUT // BANK
+PAIRS = BLOCKS // 2
+QUARTER = 2 * P
 
-WARM_START = 8
-WARM_FILL = 3
+WARM_START = 4
+WARM_FILL = 1
 
 FLOPS = 2 * ((STEPS - 1) * NODES * NODES * F_IN + (2 * STEPS - 1) * NODES * F_IN * F_OUT)
 
@@ -51,14 +53,24 @@ def tile_stgnnlayer_pa_kernel(tc, X, S, w0, w1, out):
         def load_x(t):
             nc.sync.dma_start(out=by_block(x_sb[t]), in_=by_node(X[0, t]))
 
+        def load_x_pair(t, u):
+            nc.sync.dma_start(out=by_block(x_sb[t])[:, u, :, :], in_=by_node(X[0, t])[:, u, :, :])
+
         def load_w(w, tap, h):
             rows = w[h * BANK : (h + 1) * BANK, :]
             nc.sync.dma_start(out=w_sb[tap * HALVES + h][:], in_=rows.rearrange("(c p) f -> p c f", p=P))
 
-        load_x(0)
-        load_w(w0, 0, 0)
-        load_w(w0, 0, 1)
+        def load_w_pair(w, tap, h, pair):
+            rows = w[h * BANK + pair * QUARTER : h * BANK + (pair + 1) * QUARTER, :]
+            blocks = slice(2 * pair, 2 * pair + 2)
+            nc.sync.dma_start(out=w_sb[tap * HALVES + h][:, blocks, :], in_=rows.rearrange("(c p) f -> p c f", p=P))
+
+        load_x_pair(0, 0)
+        load_x_pair(0, 1)
+        load_w_pair(w0, 0, 0, 0)
+        load_w_pair(w0, 0, 0, 1)
         nc.sync.dma_start(out=by_block(s_sb), in_=by_node(S))
+        load_w(w0, 0, 1)
         load_x(1)
         load_w(w1, 1, 0)
         load_w(w1, 1, 1)
@@ -86,64 +98,83 @@ def tile_stgnnlayer_pa_kernel(tc, X, S, w0, w1, out):
         w_codes = keep.tile([P, 2, F_PASSES, F_OUT], U32, align_bytes=64)
         w_scales = keep.tile([P, 2, F_PASSES, F_OUT], U8, align_bytes=64)
 
-        def copy_for_block(j):
-            return nc.scalar.copy if j % 2 == 0 else nc.vector.tensor_copy
+        copies = {"S": nc.scalar.copy, "V": nc.vector.tensor_copy}
 
         def quantise(grouped, codes, scales):
-            nc.vector.quantize_mx(
-                out=codes.bitcast(FP8X4),
-                scales=scales,
-                in_=grouped[:].rearrange("p c v -> p (c v)"),
+            nc.vector.quantize_mx(out=codes.bitcast(FP8X4), scales=scales, in_=grouped)
+
+        def new_group():
+            return stage.tile([P, BLOCKS * P, PACK], BF16, align_bytes=64, name="grouped")
+
+        def transpose_pair(words, pair, grouped, engine):
+            bank = psum.tile([P, BANK], F32, tag="bank")
+            planes = bank[:].rearrange("p (u b c) -> p u b c", u=2, b=2)
+            for u in range(2):
+                for b in range(2):
+                    nc.tensor.transpose(planes[:, u, b, :], words[:, 2 * pair + b, u, :], ident[:])
+            copies[engine](
+                out=grouped[:].bitcast(F32)[:, QUARTER * pair : QUARTER * (pair + 1), :],
+                in_=bank[:].rearrange("p (u c) -> p c u", u=2),
             )
 
-        def transpose_and_quantise(words, codes, scales):
-            grouped = stage.tile([P, BLOCKS * P, PACK], BF16, align_bytes=64)
-            grouped_words = grouped[:].bitcast(F32)
-            for pair in range(2):
-                bank = psum.tile([P, BANK], F32, tag="bank")
-                planes = bank[:].rearrange("p (u b c) -> p u b c", u=2, b=2)
-                for u in range(2):
-                    for b in range(2):
-                        nc.tensor.transpose(planes[:, u, b, :], words[:, 2 * pair + b, u, :], ident[:])
-                nc.scalar.copy(
-                    out=grouped_words[:, 2 * P * pair : 2 * P * (pair + 1), :],
-                    in_=bank[:].rearrange("p (u c) -> p c u", u=2),
-                )
-            quantise(grouped, codes, scales)
+        def flat(grouped, rows=slice(None)):
+            return grouped[:, rows, :].rearrange("p c v -> p (c v)")
 
         def prepare_s():
             words = s_sb[:].bitcast(F32).rearrange("p j (u q) -> p j u q", u=2)
-            transpose_and_quantise(words, s_codes[:], s_scales[:])
+            grouped = new_group()
+            for pair in range(PAIRS):
+                transpose_pair(words, pair, grouped, "S")
+            return grouped
 
-        def prepare_w(tap, h):
+        def feature_words(tile):
+            return tile[:].bitcast(F32).rearrange("p j (g u q) -> p j g u q", g=F_PASSES, u=2)
+
+        def transpose_features(tile, engines):
+            words = feature_words(tile)
+            groups = []
+            for g in range(F_PASSES):
+                grouped = new_group()
+                groups.append(grouped)
+                for pair in range(PAIRS):
+                    transpose_pair(words[:, :, g, :, :], pair, grouped, engines[PAIRS * g + pair])
+            return groups
+
+        def prepare_w(tap, h, engines):
             cols = slice(h * BANK, (h + 1) * BANK)
-            words = w_sb[tap * HALVES + h][:].bitcast(F32).rearrange("p c (g u q) -> p c g u q", g=F_PASSES, u=2)
+            groups = transpose_features(w_sb[tap * HALVES + h], engines)
             for g in range(F_PASSES):
-                transpose_and_quantise(words[:, :, g, :, :], w_codes[:, tap, g, cols], w_scales[:, tap, g, cols])
+                quantise(flat(groups[g]), w_codes[:, tap, g, cols], w_scales[:, tap, g, cols])
 
-        def prepare_x_for_taps(t):
-            words = x_sb[t][:].bitcast(F32).rearrange("p j (g u q) -> p j g u q", g=F_PASSES, u=2)
+        def quantise_x_for_taps(t, groups):
             for g in range(F_PASSES):
-                transpose_and_quantise(words[:, :, g, :, :], xf_codes[:, t, g, :], xf_scales[:, t, g, :])
+                quantise(flat(groups[g]), xf_codes[:, t, g, :], xf_scales[:, t, g, :])
+
+        def prepare_x_for_taps(t, engines):
+            quantise_x_for_taps(t, transpose_features(x_sb[t], engines))
+
+        def regroup_x_for_shift(t, g):
+            grouped = new_group()
+            nc.vector.tensor_copy(
+                out=grouped[:].rearrange("p (u e q) j -> p u e q j", u=2, e=2),
+                in_=x_sb[t][:, :, g * K_PASS : (g + 1) * K_PASS].rearrange("p j (u q e) -> p u e q j", u=2, e=2),
+            )
+            return grouped
+
+        def quantise_x_for_shift(t, g, grouped):
+            cols = slice(g * K_PASS, (g + 1) * K_PASS)
+            quantise(flat(grouped), xn_codes[:, t, cols], xn_scales[:, t, cols])
 
         def prepare_x_for_shift(t):
-            halves = []
+            groups = [regroup_x_for_shift(t, g) for g in range(F_PASSES)]
             for g in range(F_PASSES):
-                grouped = stage.tile([P, K_PASS, PACK], BF16, align_bytes=64)
-                nc.vector.tensor_copy(
-                    out=grouped[:].rearrange("p (u e q) j -> p u e q j", u=2, e=2),
-                    in_=x_sb[t][:, :, g * K_PASS : (g + 1) * K_PASS].rearrange("p j (u q e) -> p u e q j", u=2, e=2),
-                )
-                halves.append(grouped)
-            for g in range(F_PASSES):
-                cols = slice(g * K_PASS, (g + 1) * K_PASS)
-                quantise(halves[g], xn_codes[:, t, cols], xn_scales[:, t, cols])
+                quantise_x_for_shift(t, g, groups[g])
 
         def graph_shift(t):
-            halves = []
+            groups = []
             for g in range(F_PASSES):
-                grouped = stage.tile([P, NODES, PACK], BF16, align_bytes=64)
-                halves.append(grouped)
+                grouped = new_group()
+                groups.append(grouped)
                 for j in range(BLOCKS):
                     nodes = slice(j * P, (j + 1) * P)
                     bank = psum.tile([P, BANK], F32, tag="bank")
@@ -159,51 +190,93 @@ def tile_stgnnlayer_pa_kernel(tc, X, S, w0, w1, out):
                             start=True,
                             stop=True,
                         )
-                    copy_for_block(j)(out=grouped[:, nodes, :], in_=planes.rearrange("p v c -> p c v"))
+                    copies["SVSV"[j]](out=grouped[:, nodes, :], in_=planes.rearrange("p v c -> p c v"))
             for g in range(F_PASSES):
-                quantise(halves[g], z_codes[:, t, g, :], z_scales[:, t, g, :])
+                quantise(flat(groups[g]), z_codes[:, t, g, :], z_scales[:, t, g, :])
 
-        def taps(t, h):
+        def tap_passes(t, out_, nodes, cols):
+            passes = [(xf_codes[:, t, g, nodes], xf_scales[:, t, g, nodes], 0, g) for g in range(F_PASSES)]
+            if t > 0:
+                passes += [(z_codes[:, t - 1, g, nodes], z_scales[:, t - 1, g, nodes], 1, g) for g in range(F_PASSES)]
+            for i, (codes, scales, tap, g) in enumerate(passes):
+                nc.tensor.matmul_mx(
+                    out=out_,
+                    lhsT=codes.bitcast(FP8X4),
+                    lhsT_scale=scales,
+                    rhs=w_codes[:, tap, g, cols].bitcast(FP8X4),
+                    rhs_scale=w_scales[:, tap, g, cols],
+                    start=(i == 0),
+                    stop=(i == len(passes) - 1),
+                )
+
+        def taps(t, h, engines):
             cols = slice(h * BANK, (h + 1) * BANK)
             y_rows = by_node(out[0, t])
             for j in range(BLOCKS):
-                nodes = slice(j * P, (j + 1) * P)
-                passes = [(xf_codes[:, t, g, nodes], xf_scales[:, t, g, nodes], 0, g) for g in range(F_PASSES)]
-                if t > 0:
-                    passes += [
-                        (z_codes[:, t - 1, g, nodes], z_scales[:, t - 1, g, nodes], 1, g) for g in range(F_PASSES)
-                    ]
                 bank = psum.tile([P, BANK], F32, tag="bank")
-                for i, (codes, scales, tap, g) in enumerate(passes):
-                    nc.tensor.matmul_mx(
-                        out=bank[:],
-                        lhsT=codes.bitcast(FP8X4),
-                        lhsT_scale=scales,
-                        rhs=w_codes[:, tap, g, cols].bitcast(FP8X4),
-                        rhs_scale=w_scales[:, tap, g, cols],
-                        start=(i == 0),
-                        stop=(i == len(passes) - 1),
-                    )
-                y_sb = results.tile([P, BANK], F32)
-                copy_for_block(j)(out=y_sb[:], in_=bank[:])
+                tap_passes(t, bank[:], slice(j * P, (j + 1) * P), cols)
+                y_sb = results.tile([P, BANK], F32, name="y_sb")
+                copies[engines[j]](out=y_sb[:], in_=bank[:])
                 nc.sync.dma_start(out=y_rows[:, j // 2, j % 2, cols], in_=y_sb[:])
 
+        def taps_quarter(t, quarter, engines):
+            cols = slice(quarter * QUARTER, (quarter + 1) * QUARTER)
+            y_rows = by_node(out[0, t])
+            for u in range(2):
+                bank = psum.tile([P, BANK], F32, tag="bank")
+                for e in range(2):
+                    j = 2 * u + e
+                    tap_passes(t, bank[:, e * QUARTER : (e + 1) * QUARTER], slice(j * P, (j + 1) * P), cols)
+                y_sb = results.tile([P, BANK], F32, name="y_sb")
+                copies[engines[u]](out=y_sb[:], in_=bank[:])
+                nc.sync.dma_start(out=y_rows[:, u, :, cols], in_=y_sb[:].rearrange("p (e o) -> p e o", e=2))
+
         keep_clock_up(WARM_START)
-        prepare_x_for_shift(0)
-        prepare_x_for_taps(0)
+        x_words = feature_words(x_sb[0])
+        x_groups = [new_group() for g in range(F_PASSES)]
+        for pair in range(PAIRS):
+            for g in range(F_PASSES):
+                transpose_pair(x_words[:, :, g, :, :], pair, x_groups[g], "S")
+            keep_clock_up(WARM_FILL)
+        shift_groups = [regroup_x_for_shift(0, 0)]
+        quantise_x_for_taps(0, x_groups)
+
+        w_words = feature_words(w_sb[0])
+        w_groups = [new_group() for g in range(F_PASSES)]
+
+        def transpose_w_quarter(pair):
+            for g in range(F_PASSES):
+                transpose_pair(w_words[:, :, g, :, :], pair, w_groups[g], "S")
+
+        def quantise_w_quarter(pair):
+            cols = slice(pair * QUARTER, (pair + 1) * QUARTER)
+            for g in range(F_PASSES):
+                quantise(flat(w_groups[g], cols), w_codes[:, 0, g, cols], w_scales[:, 0, g, cols])
+
+        transpose_w_quarter(0)
+        quantise_w_quarter(0)
         keep_clock_up(WARM_FILL)
-        prepare_w(0, 0)
-        keep_clock_up(WARM_FILL)
-        prepare_w(0, 1)
-        keep_clock_up(WARM_FILL)
-        prepare_s()
-        for t in range(STEPS):
-            for h in range(HALVES):
-                taps(t, h)
-                if h == 0 and t + 1 < STEPS:
-                    prepare_x_for_taps(t + 1)
-                    graph_shift(t)
-                if h == 1 and t + 2 < STEPS:
-                    prepare_x_for_shift(t + 1)
-                if t == 0:
-                    prepare_w(1, h)
+        transpose_w_quarter(1)
+        taps_quarter(0, 0, "SS")
+        shift_groups.append(regroup_x_for_shift(0, 1))
+        quantise_w_quarter(1)
+        s_group = prepare_s()
+        quantise_x_for_shift(0, 0, shift_groups[0])
+        quantise(flat(s_group), s_codes[:], s_scales[:])
+        taps_quarter(0, 1, "SV")
+        quantise_x_for_shift(0, 1, shift_groups[1])
+        prepare_w(0, 1, "SSSV")
+        graph_shift(0)
+        prepare_x_for_taps(1, "SSSV")
+        taps(0, 1, "SSSV")
+        prepare_w(1, 0, "SSSV")
+        prepare_x_for_shift(1)
+        prepare_w(1, 1, "SSSV")
+        for t in range(1, STEPS):
+            taps(t, 0, "SSSV")
+            if t + 1 < STEPS:
+                prepare_x_for_taps(t + 1, "SSSV")
+                graph_shift(t)
+            taps(t, 1, "SSSV")
+            if t + 2 < STEPS:
+                prepare_x_for_shift(t + 1)

@@ -58,12 +58,15 @@ def tile_stgnnlayer_pa_kernel(tc, X, S, w0, w1, out):
 
         def load_w(w, tap, h):
             rows = w[h * BANK : (h + 1) * BANK, :]
-            nc.sync.dma_start(out=w_sb[tap * HALVES + h][:], in_=rows.rearrange("(c p) f -> p c f", p=P))
+            nc.sync.dma_start(
+                out=w_sb[tap * HALVES + h][:].rearrange("p (q c) f -> p q c f", q=PAIRS),
+                in_=rows.rearrange("(q p c) f -> p q c f", p=P, q=PAIRS),
+            )
 
         def load_w_pair(w, tap, h, pair):
             rows = w[h * BANK + pair * QUARTER : h * BANK + (pair + 1) * QUARTER, :]
             blocks = slice(2 * pair, 2 * pair + 2)
-            nc.sync.dma_start(out=w_sb[tap * HALVES + h][:, blocks, :], in_=rows.rearrange("(c p) f -> p c f", p=P))
+            nc.sync.dma_start(out=w_sb[tap * HALVES + h][:, blocks, :], in_=rows.rearrange("(p c) f -> p c f", p=P))
 
         load_x_pair(0, 0)
         load_x_pair(0, 1)
@@ -209,6 +212,12 @@ def tile_stgnnlayer_pa_kernel(tc, X, S, w0, w1, out):
                     stop=(i == len(passes) - 1),
                 )
 
+        def copy_y(engine, y_sb, bank):
+            copies[engine](
+                out=y_sb[:].rearrange("p (q r c) -> p q r c", q=2, c=2),
+                in_=bank[:].rearrange("p (q c r) -> p q r c", q=2, c=2),
+            )
+
         def taps(t, h, engines):
             cols = slice(h * BANK, (h + 1) * BANK)
             y_rows = by_node(out[0, t])
@@ -216,7 +225,7 @@ def tile_stgnnlayer_pa_kernel(tc, X, S, w0, w1, out):
                 bank = psum.tile([P, BANK], F32, tag="bank")
                 tap_passes(t, bank[:], slice(j * P, (j + 1) * P), cols)
                 y_sb = results.tile([P, BANK], F32, name="y_sb")
-                copies[engines[j]](out=y_sb[:], in_=bank[:])
+                copy_y(engines[j], y_sb, bank)
                 nc.sync.dma_start(out=y_rows[:, j // 2, j % 2, cols], in_=y_sb[:])
 
         def taps_quarter(t, quarter, engines):
@@ -228,7 +237,7 @@ def tile_stgnnlayer_pa_kernel(tc, X, S, w0, w1, out):
                     j = 2 * u + e
                     tap_passes(t, bank[:, e * QUARTER : (e + 1) * QUARTER], slice(j * P, (j + 1) * P), cols)
                 y_sb = results.tile([P, BANK], F32, name="y_sb")
-                copies[engines[u]](out=y_sb[:], in_=bank[:])
+                copy_y(engines[u], y_sb, bank)
                 nc.sync.dma_start(out=y_rows[:, u, :, cols], in_=y_sb[:].rearrange("p (e o) -> p e o", e=2))
 
         keep_clock_up(WARM_START)

@@ -214,19 +214,21 @@ def tile_stgnnlayer_pa_kernel(tc, X, S, w0, w1, out):
 
         def copy_y(engine, y_sb, bank):
             copies[engine](
-                out=y_sb[:].rearrange("p (q r c) -> p q r c", q=2, c=2),
-                in_=bank[:].rearrange("p (q c r) -> p q r c", q=2, c=2),
+                out=y_sb.rearrange("p (q r c) -> p q r c", r=P, c=2),
+                in_=bank.rearrange("p (q c r) -> p q r c", r=P, c=2),
             )
 
+        def y_block(t, j, first, width, engine):
+            cols = slice(first, first + width)
+            bank = psum.tile([P, BANK], F32, tag="bank")
+            tap_passes(t, bank[:, :width], slice(j * P, (j + 1) * P), cols)
+            y_sb = results.tile([P, BANK], F32, name="y_sb")
+            copy_y(engine, y_sb[:, :width], bank[:, :width])
+            nc.sync.dma_start(out=by_node(out[0, t])[:, j // 2, j % 2, cols], in_=y_sb[:, :width])
+
         def taps(t, h, engines):
-            cols = slice(h * BANK, (h + 1) * BANK)
-            y_rows = by_node(out[0, t])
-            for j in range(BLOCKS):
-                bank = psum.tile([P, BANK], F32, tag="bank")
-                tap_passes(t, bank[:], slice(j * P, (j + 1) * P), cols)
-                y_sb = results.tile([P, BANK], F32, name="y_sb")
-                copy_y(engines[j], y_sb, bank)
-                nc.sync.dma_start(out=y_rows[:, j // 2, j % 2, cols], in_=y_sb[:])
+            for j, engine in enumerate(engines):
+                y_block(t, j, h * BANK, BANK, engine)
 
         def taps_quarter(t, quarter, engines):
             cols = slice(quarter * QUARTER, (quarter + 1) * QUARTER)
@@ -237,7 +239,7 @@ def tile_stgnnlayer_pa_kernel(tc, X, S, w0, w1, out):
                     j = 2 * u + e
                     tap_passes(t, bank[:, e * QUARTER : (e + 1) * QUARTER], slice(j * P, (j + 1) * P), cols)
                 y_sb = results.tile([P, BANK], F32, name="y_sb")
-                copy_y(engines[u], y_sb, bank)
+                copy_y(engines[u], y_sb[:], bank[:])
                 nc.sync.dma_start(out=y_rows[:, u, :, cols], in_=y_sb[:].rearrange("p (e o) -> p e o", e=2))
 
         keep_clock_up(WARM_START)
@@ -277,15 +279,18 @@ def tile_stgnnlayer_pa_kernel(tc, X, S, w0, w1, out):
         prepare_w(0, 1, "SSSV")
         graph_shift(0)
         prepare_x_for_taps(1, "SSSV")
-        taps(0, 1, "SSSV")
+        taps(0, 1, "SSSS")
         prepare_w(1, 0, "SSSV")
         prepare_x_for_shift(1)
         prepare_w(1, 1, "SSSV")
         for t in range(1, STEPS):
-            taps(t, 0, "SSSV")
+            taps(t, 0, "SSSS")
             if t + 1 < STEPS:
                 prepare_x_for_taps(t + 1, "SSSV")
                 graph_shift(t)
-            taps(t, 1, "SSSV")
+                taps(t, 1, "SSSS")
             if t + 2 < STEPS:
                 prepare_x_for_shift(t + 1)
+        taps(STEPS - 1, 1, "SVS")
+        y_block(STEPS - 1, BLOCKS - 1, BANK, QUARTER, "S")
+        y_block(STEPS - 1, BLOCKS - 1, BANK + QUARTER, QUARTER, "V")

@@ -158,10 +158,12 @@ def tile_stgnnlayer_pa_kernel(tc, X, S, w0, w1, out):
 
         def regroup_x_for_shift(t, g):
             grouped = new_group()
-            nc.vector.tensor_copy(
-                out=grouped[:].rearrange("p (u e q) j -> p u e q j", u=2, e=2),
-                in_=x_sb[t][:, :, g * K_PASS : (g + 1) * K_PASS].rearrange("p j (u q e) -> p u e q j", u=2, e=2),
-            )
+            for u in range(2):
+                first = g * K_PASS + u * QUARTER
+                nc.vector.tensor_copy(
+                    out=grouped[:, u * QUARTER : (u + 1) * QUARTER, :].rearrange("p (e c i) j -> p e c j i", e=2, i=4),
+                    in_=x_sb[t][:, :, first : first + QUARTER].rearrange("p j (c i e) -> p e c j i", e=2, i=4),
+                )
             return grouped
 
         def quantise_x_for_shift(t, g, grouped):
@@ -178,14 +180,18 @@ def tile_stgnnlayer_pa_kernel(tc, X, S, w0, w1, out):
             for g in range(F_PASSES):
                 grouped = new_group()
                 groups.append(grouped)
-                for j in range(BLOCKS):
-                    nodes = slice(j * P, (j + 1) * P)
+                values = PACK if t == 0 else 2
+                width = BANK // values
+                for i in range(BLOCKS):
+                    half, part = divmod(i, PACK // values)
+                    nodes = slice(half * width, (half + 1) * width)
                     bank = psum.tile([P, BANK], F32, tag="bank")
-                    planes = bank[:].rearrange("p (v c) -> p v c", v=PACK)
-                    for v in range(PACK):
+                    planes = bank[:].rearrange("p (v c) -> p v c", v=values)
+                    for i_v in range(values):
+                        v = part * values + i_v
                         feats = slice(g * K_PASS + v * P, g * K_PASS + (v + 1) * P)
                         nc.tensor.matmul_mx(
-                            out=planes[:, v, :],
+                            out=planes[:, i_v, :],
                             lhsT=xn_codes[:, t, feats].bitcast(FP8X4),
                             lhsT_scale=xn_scales[:, t, feats],
                             rhs=s_codes[:, nodes].bitcast(FP8X4),
@@ -193,7 +199,8 @@ def tile_stgnnlayer_pa_kernel(tc, X, S, w0, w1, out):
                             start=True,
                             stop=True,
                         )
-                    copies["SVSV"[j]](out=grouped[:, nodes, :], in_=planes.rearrange("p v c -> p c v"))
+                    kept = slice(part * values, (part + 1) * values)
+                    copies["SVSV"[i]](out=grouped[:, nodes, kept], in_=planes.rearrange("p v c -> p c v"))
             for g in range(F_PASSES):
                 quantise(flat(groups[g]), z_codes[:, t, g, :], z_scales[:, t, g, :])
 
@@ -268,13 +275,13 @@ def tile_stgnnlayer_pa_kernel(tc, X, S, w0, w1, out):
         quantise_w_quarter(0)
         keep_clock_up(WARM_FILL)
         transpose_w_quarter(1)
-        taps_quarter(0, 0, "SS")
-        shift_groups.append(regroup_x_for_shift(0, 1))
-        quantise_w_quarter(1)
         s_group = prepare_s()
-        quantise_x_for_shift(0, 0, shift_groups[0])
+        taps_quarter(0, 0, "SS")
+        quantise_w_quarter(1)
+        shift_groups.append(regroup_x_for_shift(0, 1))
         quantise(flat(s_group), s_codes[:], s_scales[:])
-        taps_quarter(0, 1, "SV")
+        quantise_x_for_shift(0, 0, shift_groups[0])
+        taps_quarter(0, 1, "SS")
         quantise_x_for_shift(0, 1, shift_groups[1])
         prepare_w(0, 1, "SSSV")
         graph_shift(0)

@@ -23,6 +23,7 @@ F_PASSES = F_IN // K_PASS
 HALVES = F_OUT // BANK
 PAIRS = BLOCKS // 2
 QUARTER = 2 * P
+SQUARE = 32
 
 WARM_START = 4
 WARM_FILL = 1
@@ -47,7 +48,9 @@ def tile_stgnnlayer_pa_kernel(tc, X, S, w0, w1, out):
             return tile[:].rearrange("p (u e) f -> p u e f", u=2)
 
         s_sb = inputs.tile([P, BLOCKS, NODES], BF16)
-        x_sb = [inputs.tile([P, BLOCKS, F_IN], BF16, name="x_sb%d" % t) for t in range(STEPS)]
+        x_sb = [inputs.tile([P, BLOCKS, F_IN], BF16, name="x_sb%d" % t) for t in range(STEPS - 1)]
+        x_last = inputs.tile([P, NODES // SQUARE, 2 * F_PASSES, 2 * SQUARE], BF16, align_bytes=64)
+        x_turned = inputs.tile([P, NODES // SQUARE, 2 * F_PASSES, SQUARE], F32, align_bytes=64)
         w_sb = [inputs.tile([P, BLOCKS, F_IN], BF16, name="w_sb%d" % i) for i in range(2 * HALVES)]
 
         def load_x(t):
@@ -55,6 +58,15 @@ def tile_stgnnlayer_pa_kernel(tc, X, S, w0, w1, out):
 
         def load_x_pair(t, u):
             nc.sync.dma_start(out=by_block(x_sb[t])[:, u, :, :], in_=by_node(X[0, t])[:, u, :, :])
+
+        def load_x_last():
+            rows = X[0, STEPS - 1].rearrange("(r q) f -> q r f", q=SQUARE)
+            for m in range(2 * F_PASSES):
+                for a in range(P // SQUARE):
+                    first = QUARTER * m + 2 * SQUARE * a
+                    nc.sync.dma_start(
+                        out=x_last[SQUARE * a : SQUARE * (a + 1), :, m, :], in_=rows[:, :, first : first + 2 * SQUARE]
+                    )
 
         def load_w(w, tap, h):
             rows = w[h * BANK : (h + 1) * BANK, :]
@@ -78,7 +90,6 @@ def tile_stgnnlayer_pa_kernel(tc, X, S, w0, w1, out):
         load_w(w1, 1, 0)
         load_w(w1, 1, 1)
         load_x(2)
-        load_x(3)
 
         ident = keep.tile([P, P], F32)
         make_identity(nc, ident[:])
@@ -156,6 +167,23 @@ def tile_stgnnlayer_pa_kernel(tc, X, S, w0, w1, out):
         def prepare_x_for_taps(t, engines):
             quantise_x_for_taps(t, transpose_features(x_sb[t], engines))
 
+        def turn_x_last():
+            words = x_last[:].rearrange("p r m f -> p (r m f)").bitcast(F32)
+            turned = x_turned[:].rearrange("p r m q -> p (r m q)")
+            half = P * NODES // SQUARE // 2
+            for i in range(2):
+                cols = slice(i * half, (i + 1) * half)
+                nc.vector.transpose(out=turned[:, cols], in_=words[:, cols])
+
+        def regroup_x_last(groups, g, u):
+            turned = x_turned[:].rearrange("p r m (l e) -> p e r l m", e=2)
+            words = groups[g][:].bitcast(F32).rearrange("p (u e r l) m -> p u e r l m", u=2, e=2, r=8)
+            for e in range(2):
+                nc.scalar.copy(
+                    out=words[:, u, e, :, :, :],
+                    in_=turned[:, e, 8 * u : 8 * u + 8, :, 2 * g : 2 * g + 2],
+                )
+
         def regroup_x_for_shift(t, g):
             grouped = new_group()
             for u in range(2):
@@ -175,7 +203,7 @@ def tile_stgnnlayer_pa_kernel(tc, X, S, w0, w1, out):
             for g in range(F_PASSES):
                 quantise_x_for_shift(t, g, groups[g])
 
-        def graph_shift(t):
+        def graph_shift(t, engines):
             groups = []
             for g in range(F_PASSES):
                 grouped = new_group()
@@ -200,7 +228,7 @@ def tile_stgnnlayer_pa_kernel(tc, X, S, w0, w1, out):
                             stop=True,
                         )
                     kept = slice(part * values, (part + 1) * values)
-                    copies["SVSV"[i]](out=grouped[:, nodes, kept], in_=planes.rearrange("p v c -> p c v"))
+                    copies[engines[BLOCKS * g + i]](out=grouped[:, nodes, kept], in_=planes.rearrange("p v c -> p c v"))
             for g in range(F_PASSES):
                 quantise(flat(groups[g]), z_codes[:, t, g, :], z_scales[:, t, g, :])
 
@@ -284,19 +312,30 @@ def tile_stgnnlayer_pa_kernel(tc, X, S, w0, w1, out):
         taps_quarter(0, 1, "SS")
         quantise_x_for_shift(0, 1, shift_groups[1])
         prepare_w(0, 1, "SSSV")
-        graph_shift(0)
+        graph_shift(0, "SVSVSVSV")
         prepare_x_for_taps(1, "SSSV")
         taps(0, 1, "SSSS")
+        load_x_last()
         prepare_w(1, 0, "SSSV")
         prepare_x_for_shift(1)
         prepare_w(1, 1, "SSSV")
         for t in range(1, STEPS):
-            taps(t, 0, "SSSS")
-            if t + 1 < STEPS:
+            if t + 2 == STEPS:
+                x_groups = [new_group() for g in range(F_PASSES)]
+                for j in range(BLOCKS):
+                    y_block(t, j, 0, BANK, "S")
+                    regroup_x_last(x_groups, j // 2, j % 2)
+            else:
+                taps(t, 0, "SSSS")
+            if t + 2 < STEPS:
                 prepare_x_for_taps(t + 1, "SSSV")
-                graph_shift(t)
+            if t + 1 < STEPS:
+                graph_shift(t, "SVSVSVSS" if t == 1 else "SVSVSVSV")
+                if t + 2 == STEPS:
+                    quantise_x_for_taps(t + 1, x_groups)
                 taps(t, 1, "SSSS")
             if t + 2 < STEPS:
+                turn_x_last()
                 prepare_x_for_shift(t + 1)
         taps(STEPS - 1, 1, "SVS")
         y_block(STEPS - 1, BLOCKS - 1, BANK, QUARTER, "S")

@@ -15,6 +15,7 @@ K_PASS = P * PACK
 BANK = 512
 
 STEPS = 4
+TURNED = (2, 3)
 NODES = 512
 F_IN = 1024
 F_OUT = 1024
@@ -49,8 +50,10 @@ def tile_stgnnlayer_pa_kernel(tc, X, S, w0, w1, out):
 
         s_sb = inputs.tile([P, BLOCKS, NODES], BF16)
         x_sb = [inputs.tile([P, BLOCKS, F_IN], BF16, name="x_sb%d" % t) for t in range(STEPS - 1)]
-        x_last = inputs.tile([P, NODES // SQUARE, 2 * F_PASSES, 2 * SQUARE], BF16, align_bytes=64)
-        x_turned = inputs.tile([P, NODES // SQUARE, 2 * F_PASSES, SQUARE], F32, align_bytes=64)
+        raw_shape = [P, NODES // SQUARE, 2 * F_PASSES, 2 * SQUARE]
+        turned_shape = [P, NODES // SQUARE, 2 * F_PASSES, SQUARE]
+        x_raw = {t: inputs.tile(raw_shape, BF16, align_bytes=64, name="x_raw%d" % t) for t in TURNED}
+        x_turned = {t: inputs.tile(turned_shape, F32, align_bytes=64, name="x_turned%d" % t) for t in TURNED}
         w_sb = [inputs.tile([P, BLOCKS, F_IN], BF16, name="w_sb%d" % i) for i in range(2 * HALVES)]
 
         def load_x(t):
@@ -59,13 +62,13 @@ def tile_stgnnlayer_pa_kernel(tc, X, S, w0, w1, out):
         def load_x_pair(t, u):
             nc.sync.dma_start(out=by_block(x_sb[t])[:, u, :, :], in_=by_node(X[0, t])[:, u, :, :])
 
-        def load_x_last():
-            rows = X[0, STEPS - 1].rearrange("(r q) f -> q r f", q=SQUARE)
+        def load_squares(t):
+            rows = X[0, t].rearrange("(r q) f -> q r f", q=SQUARE)
             for m in range(2 * F_PASSES):
                 for a in range(P // SQUARE):
                     first = QUARTER * m + 2 * SQUARE * a
                     nc.sync.dma_start(
-                        out=x_last[SQUARE * a : SQUARE * (a + 1), :, m, :], in_=rows[:, :, first : first + 2 * SQUARE]
+                        out=x_raw[t][SQUARE * a : SQUARE * (a + 1), :, m, :], in_=rows[:, :, first : first + 2 * SQUARE]
                     )
 
         def load_w(w, tap, h):
@@ -89,6 +92,7 @@ def tile_stgnnlayer_pa_kernel(tc, X, S, w0, w1, out):
         load_x(1)
         load_w(w1, 1, 0)
         load_w(w1, 1, 1)
+        load_squares(2)
         load_x(2)
 
         ident = keep.tile([P, P], F32)
@@ -167,22 +171,26 @@ def tile_stgnnlayer_pa_kernel(tc, X, S, w0, w1, out):
         def prepare_x_for_taps(t, engines):
             quantise_x_for_taps(t, transpose_features(x_sb[t], engines))
 
-        def turn_x_last():
-            words = x_last[:].rearrange("p r m f -> p (r m f)").bitcast(F32)
-            turned = x_turned[:].rearrange("p r m q -> p (r m q)")
+        def turn(t):
+            words = x_raw[t][:].rearrange("p r m f -> p (r m f)").bitcast(F32)
+            turned = x_turned[t][:].rearrange("p r m q -> p (r m q)")
             half = P * NODES // SQUARE // 2
             for i in range(2):
                 cols = slice(i * half, (i + 1) * half)
                 nc.vector.transpose(out=turned[:, cols], in_=words[:, cols])
 
-        def regroup_x_last(groups, g, u):
-            turned = x_turned[:].rearrange("p r m (l e) -> p e r l m", e=2)
-            words = groups[g][:].bitcast(F32).rearrange("p (u e r l) m -> p u e r l m", u=2, e=2, r=8)
-            for e in range(2):
-                nc.scalar.copy(
-                    out=words[:, u, e, :, :, :],
-                    in_=turned[:, e, 8 * u : 8 * u + 8, :, 2 * g : 2 * g + 2],
-                )
+        def regroup_turned(t):
+            turned = x_turned[t][:].rearrange("p r m (l e) -> p e r l m", e=2)
+            groups = [new_group() for g in range(F_PASSES)]
+            for g in range(F_PASSES):
+                words = groups[g][:].bitcast(F32).rearrange("p (u e r l) m -> p u e r l m", u=2, e=2, r=8)
+                for u in range(2):
+                    for e in range(2):
+                        nc.scalar.copy(
+                            out=words[:, u, e, :, :, :],
+                            in_=turned[:, e, 8 * u : 8 * u + 8, :, 2 * g : 2 * g + 2],
+                        )
+            return groups
 
         def regroup_x_for_shift(t, g):
             grouped = new_group()
@@ -208,7 +216,7 @@ def tile_stgnnlayer_pa_kernel(tc, X, S, w0, w1, out):
             for g in range(F_PASSES):
                 grouped = new_group()
                 groups.append(grouped)
-                values = PACK if t == 0 else 2
+                values = PACK
                 width = BANK // values
                 for i in range(BLOCKS):
                     half, part = divmod(i, PACK // values)
@@ -232,20 +240,26 @@ def tile_stgnnlayer_pa_kernel(tc, X, S, w0, w1, out):
             for g in range(F_PASSES):
                 quantise(flat(groups[g]), z_codes[:, t, g, :], z_scales[:, t, g, :])
 
-        def tap_passes(t, out_, nodes, cols):
-            passes = [(xf_codes[:, t, g, nodes], xf_scales[:, t, g, nodes], 0, g) for g in range(F_PASSES)]
-            if t > 0:
-                passes += [(z_codes[:, t - 1, g, nodes], z_scales[:, t - 1, g, nodes], 1, g) for g in range(F_PASSES)]
-            for i, (codes, scales, tap, g) in enumerate(passes):
+        def tap_passes(t, tap, out_, nodes, cols, first, last):
+            for g in range(F_PASSES):
+                if tap == 0:
+                    codes, scales = xf_codes[:, t, g, nodes], xf_scales[:, t, g, nodes]
+                else:
+                    codes, scales = z_codes[:, t - 1, g, nodes], z_scales[:, t - 1, g, nodes]
                 nc.tensor.matmul_mx(
                     out=out_,
                     lhsT=codes.bitcast(FP8X4),
                     lhsT_scale=scales,
                     rhs=w_codes[:, tap, g, cols].bitcast(FP8X4),
                     rhs_scale=w_scales[:, tap, g, cols],
-                    start=(i == 0),
-                    stop=(i == len(passes) - 1),
+                    start=(first and g == 0),
+                    stop=(last and g == F_PASSES - 1),
                 )
+
+        def both_taps(t, out_, nodes, cols):
+            tap_passes(t, 0, out_, nodes, cols, True, t == 0)
+            if t > 0:
+                tap_passes(t, 1, out_, nodes, cols, False, True)
 
         def copy_y(engine, y_sb, bank):
             copies[engine](
@@ -256,7 +270,11 @@ def tile_stgnnlayer_pa_kernel(tc, X, S, w0, w1, out):
         def y_block(t, j, first, width, engine):
             cols = slice(first, first + width)
             bank = psum.tile([P, BANK], F32, tag="bank")
-            tap_passes(t, bank[:, :width], slice(j * P, (j + 1) * P), cols)
+            both_taps(t, bank[:, :width], slice(j * P, (j + 1) * P), cols)
+            store_y(t, j, first, width, engine, bank)
+
+        def store_y(t, j, first, width, engine, bank):
+            cols = slice(first, first + width)
             y_sb = results.tile([P, BANK], F32, name="y_sb")
             copy_y(engine, y_sb[:, :width], bank[:, :width])
             nc.sync.dma_start(out=by_node(out[0, t])[:, j // 2, j % 2, cols], in_=y_sb[:, :width])
@@ -265,6 +283,17 @@ def tile_stgnnlayer_pa_kernel(tc, X, S, w0, w1, out):
             for j, engine in enumerate(engines):
                 y_block(t, j, h * BANK, BANK, engine)
 
+        def taps_shift_first(t, h, engines):
+            cols = slice(h * BANK, (h + 1) * BANK)
+            banks = []
+            for j in range(BLOCKS):
+                bank = psum.tile([P, BANK], F32, tag="bank")
+                banks.append(bank)
+                tap_passes(t, 1, bank[:], slice(j * P, (j + 1) * P), cols, True, False)
+            for j, engine in enumerate(engines):
+                tap_passes(t, 0, banks[j][:], slice(j * P, (j + 1) * P), cols, False, True)
+                store_y(t, j, h * BANK, BANK, engine, banks[j])
+
         def taps_quarter(t, quarter, engines):
             cols = slice(quarter * QUARTER, (quarter + 1) * QUARTER)
             y_rows = by_node(out[0, t])
@@ -272,7 +301,7 @@ def tile_stgnnlayer_pa_kernel(tc, X, S, w0, w1, out):
                 bank = psum.tile([P, BANK], F32, tag="bank")
                 for e in range(2):
                     j = 2 * u + e
-                    tap_passes(t, bank[:, e * QUARTER : (e + 1) * QUARTER], slice(j * P, (j + 1) * P), cols)
+                    both_taps(t, bank[:, e * QUARTER : (e + 1) * QUARTER], slice(j * P, (j + 1) * P), cols)
                 y_sb = results.tile([P, BANK], F32, name="y_sb")
                 copy_y(engines[u], y_sb[:], bank[:])
                 nc.sync.dma_start(out=y_rows[:, u, :, cols], in_=y_sb[:].rearrange("p (e o) -> p e o", e=2))
@@ -315,28 +344,20 @@ def tile_stgnnlayer_pa_kernel(tc, X, S, w0, w1, out):
         graph_shift(0, "SVSVSVSV")
         prepare_x_for_taps(1, "SSSV")
         taps(0, 1, "SSSS")
-        load_x_last()
+        load_squares(3)
         prepare_w(1, 0, "SSSV")
         prepare_x_for_shift(1)
         prepare_w(1, 1, "SSSV")
+        turn(2)
         for t in range(1, STEPS):
-            if t + 2 == STEPS:
-                x_groups = [new_group() for g in range(F_PASSES)]
-                for j in range(BLOCKS):
-                    y_block(t, j, 0, BANK, "S")
-                    regroup_x_last(x_groups, j // 2, j % 2)
-            else:
-                taps(t, 0, "SSSS")
-            if t + 2 < STEPS:
-                prepare_x_for_taps(t + 1, "SSSV")
+            (taps_shift_first if t in TURNED else taps)(t, 0, "SSSS")
             if t + 1 < STEPS:
-                graph_shift(t, "SVSVSVSS" if t == 1 else "SVSVSVSV")
-                if t + 2 == STEPS:
-                    quantise_x_for_taps(t + 1, x_groups)
+                graph_shift(t, "SVSVSVSV")
+                quantise_x_for_taps(t + 1, regroup_turned(t + 1))
                 taps(t, 1, "SSSS")
             if t + 2 < STEPS:
-                turn_x_last()
                 prepare_x_for_shift(t + 1)
+                turn(t + 2)
         taps(STEPS - 1, 1, "SVS")
         y_block(STEPS - 1, BLOCKS - 1, BANK, QUARTER, "S")
         y_block(STEPS - 1, BLOCKS - 1, BANK + QUARTER, QUARTER, "V")

@@ -237,6 +237,9 @@ def tile_stgnnlayer_pa_kernel(tc, X, S, w0, w1, out):
                         )
                     kept = slice(part * values, (part + 1) * values)
                     copies[engines[BLOCKS * g + i]](out=grouped[:, nodes, kept], in_=planes.rearrange("p v c -> p c v"))
+            return groups
+
+        def quantise_z(t, groups):
             for g in range(F_PASSES):
                 quantise(flat(groups[g]), z_codes[:, t, g, :], z_scales[:, t, g, :])
 
@@ -339,25 +342,25 @@ def tile_stgnnlayer_pa_kernel(tc, X, S, w0, w1, out):
         quantise(flat(s_group), s_codes[:], s_scales[:])
         quantise_x_for_shift(0, 0, shift_groups[0])
         taps_quarter(0, 1, "SS")
+        load_squares(3)
         quantise_x_for_shift(0, 1, shift_groups[1])
         prepare_w(0, 1, "SSSV")
-        graph_shift(0, "SVSVSVSV")
+        quantise_z(0, graph_shift(0, "SVSVSVSV"))
         prepare_x_for_taps(1, "SSSV")
         taps(0, 1, "SSSS")
-        load_squares(3)
         prepare_w(1, 0, "SSSV")
         prepare_x_for_shift(1)
         prepare_w(1, 1, "SSSV")
-        turn(2)
         for t in range(1, STEPS):
             (taps_shift_first if t in TURNED else taps)(t, 0, "SSSS")
             if t + 1 < STEPS:
-                graph_shift(t, "SVSVSVSV")
+                z_groups = graph_shift(t, "SVSSSVSS")
+                turn(t + 1)
+                quantise_z(t, z_groups)
                 quantise_x_for_taps(t + 1, regroup_turned(t + 1))
                 taps(t, 1, "SSSS")
             if t + 2 < STEPS:
                 prepare_x_for_shift(t + 1)
-                turn(t + 2)
         taps(STEPS - 1, 1, "SVS")
         y_block(STEPS - 1, BLOCKS - 1, BANK, QUARTER, "S")
         y_block(STEPS - 1, BLOCKS - 1, BANK + QUARTER, QUARTER, "V")

from contextlib import ExitStack

import concourse.mybir as mybir
from concourse.masks import make_identity

BF16 = mybir.dt.bfloat16
F32 = mybir.dt.float32
U32 = mybir.dt.uint32
U8 = mybir.dt.uint8
FP8X4 = mybir.dt.float8_e4m3fn_x4

P = 128
PACK = 4
K_PASS = P * PACK
BANK = 512

STEPS = 4
TURNED = (2, 3)
NODES = 512
F_IN = 1024
F_OUT = 1024
BLOCKS = NODES // P
F_PASSES = F_IN // K_PASS
HALVES = F_OUT // BANK
PAIRS = BLOCKS // 2
QUARTER = 2 * P
SQUARE = 32

WARM_START = 4
WARM_FILL = 1

FLOPS = 2 * ((STEPS - 1) * NODES * NODES * F_IN + (2 * STEPS - 1) * NODES * F_IN * F_OUT)


def tile_stgnnlayer_pa_kernel(tc, X, S, w0, w1, out):
    nc = tc.nc
    with ExitStack() as ctx:
        inputs = ctx.enter_context(tc.tile_pool(name="inputs", bufs=1))
        keep = ctx.enter_context(tc.tile_pool(name="keep", bufs=1))
        stage = ctx.enter_context(tc.tile_pool(name="stage", bufs=8))
        results = ctx.enter_context(tc.tile_pool(name="results", bufs=16))
        psum = ctx.enter_context(tc.psum_pool(name="psum", bufs=8))
        ctx.enter_context(tc.manual_schedule())

        def by_node(matrix):
            return matrix.rearrange("(u p e) f -> p u e f", u=2, e=2)

        def by_block(tile):
            return tile[:].rearrange("p (u e) f -> p u e f", u=2)

        s_sb = inputs.tile([P, BLOCKS, NODES], BF16)
        x_sb = [inputs.tile([P, BLOCKS, F_IN], BF16, name="x_sb%d" % t) for t in range(STEPS - 1)]
        raw_shape = [P, NODES // SQUARE, 2 * F_PASSES, 2 * SQUARE]
        turned_shape = [P, NODES // SQUARE, 2 * F_PASSES, SQUARE]
        x_raw = {t: inputs.tile(raw_shape, BF16, align_bytes=64, name="x_raw%d" % t) for t in TURNED}
        x_turned = {t: inputs.tile(turned_shape, F32, align_bytes=64, name="x_turned%d" % t) for t in TURNED}
        w_sb = [inputs.tile([P, BLOCKS, F_IN], BF16, name="w_sb%d" % i) for i in range(2 * HALVES)]

        def load_x(t):
            nc.sync.dma_start(out=by_block(x_sb[t]), in_=by_node(X[0, t]))

        def load_x_pair(t, u):
            nc.sync.dma_start(out=by_block(x_sb[t])[:, u, :, :], in_=by_node(X[0, t])[:, u, :, :])

        def load_squares(t):
            rows = X[0, t].rearrange("(r q) f -> q r f", q=SQUARE)
            for m in range(2 * F_PASSES):
                for a in range(P // SQUARE):
                    first = QUARTER * m + 2 * SQUARE * a
                    nc.sync.dma_start(
                        out=x_raw[t][SQUARE * a : SQUARE * (a + 1), :, m, :], in_=rows[:, :, first : first + 2 * SQUARE]
                    )

        def load_w(w, tap, h):
            rows = w[h * BANK : (h + 1) * BANK, :]
            nc.sync.dma_start(
                out=w_sb[tap * HALVES + h][:].rearrange("p (q c) f -> p q c f", q=PAIRS),
                in_=rows.rearrange("(q p c) f -> p q c f", p=P, q=PAIRS),
            )

        def load_w_pair(w, tap, h, pair):
            rows = w[h * BANK + pair * QUARTER : h * BANK + (pair + 1) * QUARTER, :]
            blocks = slice(2 * pair, 2 * pair + 2)
            nc.sync.dma_start(out=w_sb[tap * HALVES + h][:, blocks, :], in_=rows.rearrange("(p c) f -> p c f", p=P))

        load_x_pair(0, 0)
        load_x_pair(0, 1)
        load_w_pair(w0, 0, 0, 0)
        load_w_pair(w0, 0, 0, 1)
        nc.sync.dma_start(out=by_block(s_sb), in_=by_node(S))
        load_w(w0, 0, 1)
        load_x(1)
        load_w(w1, 1, 0)
        load_w(w1, 1, 1)
        load_squares(2)
        load_x(2)

        ident = keep.tile([P, P], F32)
        make_identity(nc, ident[:])
        zeros = keep.tile([P, BANK], BF16)
        nc.vector.memset(zeros[:], 0.0)

        def keep_clock_up(count):
            unread = psum.tile([P, BANK], F32, tag="bank")
            for i in range(count):
                nc.tensor.matmul(out=unread[:], lhsT=zeros[:, :P], rhs=zeros[:], start=True, stop=True)

        s_codes = keep.tile([P, NODES], U32, align_bytes=64)
        s_scales = keep.tile([P, NODES], U8, align_bytes=64)
        xn_codes = keep.tile([P, STEPS - 1, F_IN], U32, align_bytes=64)
        xn_scales = keep.tile([P, STEPS - 1, F_IN], U8, align_bytes=64)
        xf_codes = keep.tile([P, STEPS, F_PASSES, NODES], U32, align_bytes=64)
        xf_scales = keep.tile([P, STEPS, F_PASSES, NODES], U8, align_bytes=64)
        z_codes = keep.tile([P, STEPS - 1, F_PASSES, NODES], U32, align_bytes=64)
        z_scales = keep.tile([P, STEPS - 1, F_PASSES, NODES], U8, align_bytes=64)
        w_codes = keep.tile([P, 2, F_PASSES, F_OUT], U32, align_bytes=64)
        w_scales = keep.tile([P, 2, F_PASSES, F_OUT], U8, align_bytes=64)

        copies = {"S": nc.scalar.copy, "V": nc.vector.tensor_copy}

        def quantise(grouped, codes, scales):
            nc.vector.quantize_mx(out=codes.bitcast(FP8X4), scales=scales, in_=grouped)

        def new_group():
            return stage.tile([P, BLOCKS * P, PACK], BF16, align_bytes=64, name="grouped")

        def transpose_pair(words, pair, grouped, engine):
            bank = psum.tile([P, BANK], F32, tag="bank")
            planes = bank[:].rearrange("p (u b c) -> p u b c", u=2, b=2)
            for u in range(2):
                for b in range(2):
                    nc.tensor.transpose(planes[:, u, b, :], words[:, 2 * pair + b, u, :], ident[:])
            copies[engine](
                out=grouped[:].bitcast(F32)[:, QUARTER * pair : QUARTER * (pair + 1), :],
                in_=bank[:].rearrange("p (u c) -> p c u", u=2),
            )

        def flat(grouped, rows=slice(None)):
            return grouped[:, rows, :].rearrange("p c v -> p (c v)")

        def prepare_s():
            words = s_sb[:].bitcast(F32).rearrange("p j (u q) -> p j u q", u=2)
            grouped = new_group()
            for pair in range(PAIRS):
                transpose_pair(words, pair, grouped, "S")
            return grouped

        def feature_words(tile):
            return tile[:].bitcast(F32).rearrange("p j (g u q) -> p j g u q", g=F_PASSES, u=2)

        def transpose_features(tile, engines):
            words = feature_words(tile)
            groups = []
            for g in range(F_PASSES):
                grouped = new_group()
                groups.append(grouped)
                for pair in range(PAIRS):
                    transpose_pair(words[:, :, g, :, :], pair, grouped, engines[PAIRS * g + pair])
            return groups

        def prepare_w(tap, h, engines):
            cols = slice(h * BANK, (h + 1) * BANK)
            groups = transpose_features(w_sb[tap * HALVES + h], engines)
            for g in range(F_PASSES):
                quantise(flat(groups[g]), w_codes[:, tap, g, cols], w_scales[:, tap, g, cols])

        def quantise_x_for_taps(t, groups):
            for g in range(F_PASSES):
                quantise(flat(groups[g]), xf_codes[:, t, g, :], xf_scales[:, t, g, :])

        def prepare_x_for_taps(t, engines):
            quantise_x_for_taps(t, transpose_features(x_sb[t], engines))

        def turn(t):
            words = x_raw[t][:].rearrange("p r m f -> p (r m f)").bitcast(F32)
            turned = x_turned[t][:].rearrange("p r m q -> p (r m q)")
            half = P * NODES // SQUARE // 2
            for i in range(2):
                cols = slice(i * half, (i + 1) * half)
                nc.vector.transpose(out=turned[:, cols], in_=words[:, cols])

        def regroup_turned(t):
            turned = x_turned[t][:].rearrange("p r m (l e) -> p e r l m", e=2)
            groups = [new_group() for g in range(F_PASSES)]
            for g in range(F_PASSES):
                words = groups[g][:].bitcast(F32).rearrange("p (u e r l) m -> p u e r l m", u=2, e=2, r=8)
                for u in range(2):
                    for e in range(2):
                        nc.scalar.copy(
                            out=words[:, u, e, :, :, :],
                            in_=turned[:, e, 8 * u : 8 * u + 8, :, 2 * g : 2 * g + 2],
                        )
            return groups

        def regroup_x_for_shift(t, g):
            grouped = new_group()
            for u in range(2):
                first = g * K_PASS + u * QUARTER
                nc.vector.tensor_copy(
                    out=grouped[:, u * QUARTER : (u + 1) * QUARTER, :].rearrange("p (e c i) j -> p e c j i", e=2, i=4),
                    in_=x_sb[t][:, :, first : first + QUARTER].rearrange("p j (c i e) -> p e c j i", e=2, i=4),
                )
            return grouped

        def quantise_x_for_shift(t, g, grouped):
            cols = slice(g * K_PASS, (g + 1) * K_PASS)
            quantise(flat(grouped), xn_codes[:, t, cols], xn_scales[:, t, cols])

        def prepare_x_for_shift(t):
            groups = [regroup_x_for_shift(t, g) for g in range(F_PASSES)]
            for g in range(F_PASSES):
                quantise_x_for_shift(t, g, groups[g])

        def graph_shift(t, engines):
            groups = []
            for g in range(F_PASSES):
                grouped = new_group()
                groups.append(grouped)
                values = PACK
                width = BANK // values
                for i in range(BLOCKS):
                    half, part = divmod(i, PACK // values)
                    nodes = slice(half * width, (half + 1) * width)
                    bank = psum.tile([P, BANK], F32, tag="bank")
                    planes = bank[:].rearrange("p (v c) -> p v c", v=values)
                    for i_v in range(values):
                        v = part * values + i_v
                        feats = slice(g * K_PASS + v * P, g * K_PASS + (v + 1) * P)
                        nc.tensor.matmul_mx(
                            out=planes[:, i_v, :],
                            lhsT=xn_codes[:, t, feats].bitcast(FP8X4),
                            lhsT_scale=xn_scales[:, t, feats],
                            rhs=s_codes[:, nodes].bitcast(FP8X4),
                            rhs_scale=s_scales[:, nodes],
                            start=True,
                            stop=True,
                        )
                    kept = slice(part * values, (part + 1) * values)
                    copies[engines[BLOCKS * g + i]](out=grouped[:, nodes, kept], in_=planes.rearrange("p v c -> p c v"))
            return groups

        def quantise_z(t, groups):
            for g in range(F_PASSES):
                quantise(flat(groups[g]), z_codes[:, t, g, :], z_scales[:, t, g, :])

        def tap_passes(t, tap, out_, nodes, cols, first, last):
            for g in range(F_PASSES):
                if tap == 0:
                    codes, scales = xf_codes[:, t, g, nodes], xf_scales[:, t, g, nodes]
                else:
                    codes, scales = z_codes[:, t - 1, g, nodes], z_scales[:, t - 1, g, nodes]
                nc.tensor.matmul_mx(
                    out=out_,
                    lhsT=codes.bitcast(FP8X4),
                    lhsT_scale=scales,
                    rhs=w_codes[:, tap, g, cols].bitcast(FP8X4),
                    rhs_scale=w_scales[:, tap, g, cols],
                    start=(first and g == 0),
                    stop=(last and g == F_PASSES - 1),
                )

        def both_taps(t, out_, nodes, cols):
            tap_passes(t, 0, out_, nodes, cols, True, t == 0)
            if t > 0:
                tap_passes(t, 1, out_, nodes, cols, False, True)

        def copy_y(engine, y_sb, bank):
            copies[engine](
                out=y_sb.rearrange("p (q r c) -> p q r c", r=P, c=2),
                in_=bank.rearrange("p (q c r) -> p q r c", r=P, c=2),
            )

        def y_block(t, j, first, width, engine):
            cols = slice(first, first + width)
            bank = psum.tile([P, BANK], F32, tag="bank")
            both_taps(t, bank[:, :width], slice(j * P, (j + 1) * P), cols)
            store_y(t, j, first, width, engine, bank)

        def store_y(t, j, first, width, engine, bank):
            cols = slice(first, first + width)
            y_sb = results.tile([P, BANK], F32, name="y_sb")
            copy_y(engine, y_sb[:, :width], bank[:, :width])
            nc.sync.dma_start(out=by_node(out[0, t])[:, j // 2, j % 2, cols], in_=y_sb[:, :width])

        def taps(t, h, engines):
            for j, engine in enumerate(engines):
                y_block(t, j, h * BANK, BANK, engine)

        def taps_shift_first(t, h, engines):
            cols = slice(h * BANK, (h + 1) * BANK)
            banks = []
            for j in range(BLOCKS):
                bank = psum.tile([P, BANK], F32, tag="bank")
                banks.append(bank)
                tap_passes(t, 1, bank[:], slice(j * P, (j + 1) * P), cols, True, False)
            for j, engine in enumerate(engines):
                tap_passes(t, 0, banks[j][:], slice(j * P, (j + 1) * P), cols, False, True)
                store_y(t, j, h * BANK, BANK, engine, banks[j])

        def taps_quarter(t, quarter, engines):
            cols = slice(quarter * QUARTER, (quarter + 1) * QUARTER)
            y_rows = by_node(out[0, t])
            for u in range(2):
                bank = psum.tile([P, BANK], F32, tag="bank")
                for e in range(2):
                    j = 2 * u + e
                    both_taps(t, bank[:, e * QUARTER : (e + 1) * QUARTER], slice(j * P, (j + 1) * P), cols)
                y_sb = results.tile([P, BANK], F32, name="y_sb")
                copy_y(engines[u], y_sb[:], bank[:])
                nc.sync.dma_start(out=y_rows[:, u, :, cols], in_=y_sb[:].rearrange("p (e o) -> p e o", e=2))

        keep_clock_up(WARM_START)
        x_words = feature_words(x_sb[0])
        x_groups = [new_group() for g in range(F_PASSES)]
        for pair in range(PAIRS):
            for g in range(F_PASSES):
                transpose_pair(x_words[:, :, g, :, :], pair, x_groups[g], "S")
            keep_clock_up(WARM_FILL)
        shift_groups = [regroup_x_for_shift(0, 0)]
        quantise_x_for_taps(0, x_groups)

        w_words = feature_words(w_sb[0])
        w_groups = [new_group() for g in range(F_PASSES)]

        def transpose_w_quarter(pair):
            for g in range(F_PASSES):
                transpose_pair(w_words[:, :, g, :, :], pair, w_groups[g], "S")

        def quantise_w_quarter(pair):
            cols = slice(pair * QUARTER, (pair + 1) * QUARTER)
            for g in range(F_PASSES):
                quantise(flat(w_groups[g], cols), w_codes[:, 0, g, cols], w_scales[:, 0, g, cols])

        transpose_w_quarter(0)
        quantise_w_quarter(0)
        keep_clock_up(WARM_FILL)
        transpose_w_quarter(1)
        s_group = prepare_s()
        taps_quarter(0, 0, "SS")
        quantise_w_quarter(1)
        shift_groups.append(regroup_x_for_shift(0, 1))
        quantise(flat(s_group), s_codes[:], s_scales[:])
        quantise_x_for_shift(0, 0, shift_groups[0])
        taps_quarter(0, 1, "SS")
        load_squares(3)
        quantise_x_for_shift(0, 1, shift_groups[1])
        prepare_w(0, 1, "SSSV")
        quantise_z(0, graph_shift(0, "SVSVSVSV"))
        prepare_x_for_taps(1, "SSSV")
        taps(0, 1, "SSSS")
        prepare_w(1, 0, "SSSV")
        prepare_x_for_shift(1)
        prepare_w(1, 1, "SSSV")
        for t in range(1, STEPS):
            (taps_shift_first if t in TURNED else taps)(t, 0, "SSSS")
            if t + 1 < STEPS:
                z_groups = graph_shift(t, "SVSSSVSS")
                turn(t + 1)
                quantise_z(t, z_groups)
                quantise_x_for_taps(t + 1, regroup_turned(t + 1))
                taps(t, 1, "SSSS")
            if t + 2 < STEPS:
                prepare_x_for_shift(t + 1)
        taps(STEPS - 1, 1, "SVS")
        y_block(STEPS - 1, BLOCKS - 1, BANK, QUARTER, "S")
        y_block(STEPS - 1, BLOCKS - 1, BANK + QUARTER, QUARTER, "V")
